import numpy as np
import ml_dtypes


def mxq(x, axis, fmt="e4m3"):
    dtype, down = {"e4m3": (ml_dtypes.float8_e4m3fn, 7), "e5m2": (ml_dtypes.float8_e5m2, 14)}[fmt]
    v = np.moveaxis(np.asarray(x, np.float32).astype(ml_dtypes.bfloat16).astype(np.float64), axis, -1)
    blocks = v.reshape(v.shape[:-1] + (-1, 32))
    amax = np.abs(blocks).max(-1, keepdims=True)
    byte = np.maximum(np.where(amax > 0, np.frexp(amax)[1] - 1 + 127, 0) - down, 1)
    scale = np.exp2(byte - 127.0)
    codes = (blocks / scale).astype(np.float32).astype(dtype).astype(np.float64)
    return np.moveaxis((codes * scale).reshape(v.shape), -1, axis)


WIDE = False


def mx_kscale(k):
    if not WIDE:
        return np.ones(k)
    levels = np.array([20, -20, 10, -10, 0])
    a = np.random.permutation(np.resize(levels, k // 512 * 4)).reshape(k // 512, 4)
    idx = np.arange(k)
    return np.exp2(a[idx // 512, idx % 128 // 32])


BF16 = ml_dtypes.bfloat16


def bf(x):
    return np.asarray(x, np.float32).astype(BF16)


def f64(x):
    return np.asarray(x).astype(np.float64)


NUM_PLANES = 80
BOARD = 8 * 8
IN_DIM = NUM_PLANES * BOARD
OUT_DIM = 1024
B = 512


def setup_inputs():
    s = mx_kscale(B)
    x = np.random.standard_normal((B, NUM_PLANES, 8, 8)) * s[:, None, None, None]
    rows = np.random.randint(0, IN_DIM, size=OUT_DIM)
    m = np.random.standard_normal((IN_DIM, OUT_DIM)) * 0.01
    m[rows, np.arange(OUT_DIM)] += 1.0
    g = np.random.standard_normal((B, OUT_DIM)) * np.exp2(np.random.randint(-12, 1, (B, 1))) / s[:, None]
    return {"x": bf(x), "fc1": bf(m), "grad_out": bf(g)}


def reference(x, fc1, grad_out):
    h = f64(x).reshape(-1, IN_DIM)
    return mxq(h, 0, "e4m3").T @ mxq(f64(grad_out), 0, "e5m2")

@@ -1,0 +1,121 @@
+from contextlib import ExitStack
+
+import concourse.mybir as mybir
+
+BF16 = mybir.dt.bfloat16
+F32 = mybir.dt.float32
+U32 = mybir.dt.uint32
+U8 = mybir.dt.uint8
+E4M3X4 = mybir.dt.float8_e4m3fn_x4
+E5M2X4 = mybir.dt.float8_e5m2_x4
+
+P = 128
+PACK = 4
+K = 512
+IN_DIM = 5120
+OUT_DIM = 1024
+N_TILE = 512
+ROWS = 4
+BLOCK = P * ROWS
+N_BLOCKS = IN_DIM // BLOCK
+CHUNKS = (512, 1536, 3072)
+VECTOR_BANKS = (3, 7)
+
+FLOPS = 2 * K * IN_DIM * OUT_DIM
+BYTES = 2 * K * IN_DIM + 2 * K * OUT_DIM + 4 * IN_DIM * OUT_DIM
+
+
+def tile_applypolicymap_kernel(tc, x, fc1, grad_out, out):
+    nc = tc.nc
+    h_view = x.rearrange("(p j) c y z -> p j (c y z)", j=PACK)
+    g_view = grad_out.rearrange("(p j) n -> p j n", j=PACK)
+    out_view = out.rearrange("(b i r) n -> b i r n", i=P, r=ROWS)
+
+    with ExitStack() as ctx:
+        raw = ctx.enter_context(tc.tile_pool(name="raw", bufs=1))
+        grp = ctx.enter_context(tc.tile_pool(name="grp", bufs=4))
+        keep = ctx.enter_context(tc.tile_pool(name="keep", bufs=1))
+        stage = ctx.enter_context(tc.tile_pool(name="stage", bufs=7))
+        psum = ctx.enter_context(tc.psum_pool(name="psum", bufs=8))
+
+        g_raw = raw.tile([P, PACK, OUT_DIM], BF16, name="g_raw")
+        nc.sync.dma_start(out=g_raw[:], in_=g_view)
+        h_raw = []
+        first = 0
+        for c, width in enumerate(CHUNKS):
+            piece = raw.tile([P, PACK, width], BF16, name="h_raw%d" % c)
+            nc.sync.dma_start(out=piece[:], in_=h_view[:, :, first : first + width])
+            for b in range(width // BLOCK):
+                h_raw.append(piece[:, :, b * BLOCK : (b + 1) * BLOCK])
+            first += width
+
+        g_codes = keep.tile([P, OUT_DIM], U32, name="g_codes", align_bytes=64)
+        g_scales = keep.tile([P, OUT_DIM], U8, name="g_scales", align_bytes=64)
+        h_codes = []
+        h_scales = []
+        for b in range(N_BLOCKS):
+            h_codes.append(keep.tile([P, BLOCK], U32, name="h_codes%d" % b, align_bytes=64))
+            h_scales.append(keep.tile([P, BLOCK], U8, name="h_scales%d" % b, align_bytes=64))
+
+        def regroup_g(engine_copy, half):
+            grouped = grp.tile([P, N_TILE, PACK], BF16, name="grouped", tag="grouped", align_bytes=64)
+            engine_copy(
+                out=grouped[:].rearrange("p (c i) t -> p c t i", i=4),
+                in_=g_raw[:, :, half * N_TILE : (half + 1) * N_TILE].rearrange("p t (c i) -> p c t i", i=4),
+            )
+            return grouped
+
+        def quantise_g(grouped, half):
+            cols = slice(half * N_TILE, (half + 1) * N_TILE)
+            nc.vector.quantize_mx(
+                out=g_codes[:, cols].bitcast(E5M2X4),
+                scales=g_scales[:, cols],
+                in_=grouped[:].rearrange("p w t -> p (w t)"),
+            )
+
+        def regroup_h(b):
+            grouped = grp.tile([P, ROWS, P, PACK], BF16, name="grouped", tag="grouped", align_bytes=64)
+            nc.vector.tensor_copy(
+                out=grouped[:].rearrange("p r i t -> p i t r"),
+                in_=h_raw[b].rearrange("p t (i r) -> p i t r", r=ROWS),
+            )
+            return grouped
+
+        def quantise_h(grouped, b):
+            nc.vector.quantize_mx(
+                out=h_codes[b][:].bitcast(E4M3X4),
+                scales=h_scales[b][:],
+                in_=grouped[:].rearrange("p r i t -> p (r i t)"),
+            )
+
+        g0 = regroup_g(nc.vector.tensor_copy, 0)
+        g1 = regroup_g(nc.scalar.copy, 1)
+        nxt = regroup_h(0)
+        quantise_g(g0, 0)
+        quantise_h(nxt, 0)
+        quantise_g(g1, 1)
+
+        for b in range(N_BLOCKS):
+            result = stage.tile([P, ROWS, OUT_DIM], F32, name="result", tag="result")
+            if b + 1 < N_BLOCKS:
+                nxt = regroup_h(b + 1)
+            for r in range(ROWS):
+                for n in range(OUT_DIM // N_TILE):
+                    acc = psum.tile([P, N_TILE], F32, name="acc", tag="acc")
+                    nc.tensor.matmul_mx(
+                        out=acc[:],
+                        lhsT=h_codes[b][:, r * P : (r + 1) * P].bitcast(E4M3X4),
+                        lhsT_scale=h_scales[b][:, r * P : (r + 1) * P],
+                        rhs=g_codes[:, n * N_TILE : (n + 1) * N_TILE].bitcast(E5M2X4),
+                        rhs_scale=g_scales[:, n * N_TILE : (n + 1) * N_TILE],
+                        start=True,
+                        stop=True,
+                    )
+                    dst = result[:, r, n * N_TILE : (n + 1) * N_TILE]
+                    if 2 * r + n in VECTOR_BANKS:
+                        nc.vector.tensor_copy(out=dst, in_=acc[:])
+                    else:
+                        nc.scalar.copy(out=dst, in_=acc[:])
+                if r == 1 and b + 1 < N_BLOCKS:
+                    quantise_h(nxt, b + 1)
+            nc.sync.dma_start(out=out_view[b], in_=result[:])

@@ -118,4 +118,7 @@ def tile_applypolicymap_kernel(tc, x, fc1, grad_out, out):
                         nc.scalar.copy(out=dst, in_=acc[:])
                 if r == 1 and b + 1 < N_BLOCKS:
                     quantise_h(nxt, b + 1)
-            nc.sync.dma_start(out=out_view[b], in_=result[:])
+                if b == 0:
+                    nc.sync.dma_start(out=out_view[b][:, r, :], in_=result[:, r, :])
+            if b > 0:
+                nc.sync.dma_start(out=out_view[b], in_=result[:])

from contextlib import ExitStack

import concourse.mybir as mybir

BF16 = mybir.dt.bfloat16
F32 = mybir.dt.float32
U32 = mybir.dt.uint32
U8 = mybir.dt.uint8
E4M3X4 = mybir.dt.float8_e4m3fn_x4
E5M2X4 = mybir.dt.float8_e5m2_x4

P = 128
PACK = 4
K = 512
IN_DIM = 5120
OUT_DIM = 1024
N_TILE = 512
ROWS = 4
BLOCK = P * ROWS
N_BLOCKS = IN_DIM // BLOCK
CHUNKS = (512, 1536, 3072)
VECTOR_BANKS = (3, 7)

FLOPS = 2 * K * IN_DIM * OUT_DIM
BYTES = 2 * K * IN_DIM + 2 * K * OUT_DIM + 4 * IN_DIM * OUT_DIM


def tile_applypolicymap_kernel(tc, x, fc1, grad_out, out):
    nc = tc.nc
    h_view = x.rearrange("(p j) c y z -> p j (c y z)", j=PACK)
    g_view = grad_out.rearrange("(p j) n -> p j n", j=PACK)
    out_view = out.rearrange("(b i r) n -> b i r n", i=P, r=ROWS)

    with ExitStack() as ctx:
        raw = ctx.enter_context(tc.tile_pool(name="raw", bufs=1))
        grp = ctx.enter_context(tc.tile_pool(name="grp", bufs=4))
        keep = ctx.enter_context(tc.tile_pool(name="keep", bufs=1))
        stage = ctx.enter_context(tc.tile_pool(name="stage", bufs=7))
        psum = ctx.enter_context(tc.psum_pool(name="psum", bufs=8))

        g_raw = raw.tile([P, PACK, OUT_DIM], BF16, name="g_raw")
        nc.sync.dma_start(out=g_raw[:], in_=g_view)
        h_raw = []
        first = 0
        for c, width in enumerate(CHUNKS):
            piece = raw.tile([P, PACK, width], BF16, name="h_raw%d" % c)
            nc.sync.dma_start(out=piece[:], in_=h_view[:, :, first : first + width])
            for b in range(width // BLOCK):
                h_raw.append(piece[:, :, b * BLOCK : (b + 1) * BLOCK])
            first += width

        g_codes = keep.tile([P, OUT_DIM], U32, name="g_codes", align_bytes=64)
        g_scales = keep.tile([P, OUT_DIM], U8, name="g_scales", align_bytes=64)
        h_codes = []
        h_scales = []
        for b in range(N_BLOCKS):
            h_codes.append(keep.tile([P, BLOCK], U32, name="h_codes%d" % b, align_bytes=64))
            h_scales.append(keep.tile([P, BLOCK], U8, name="h_scales%d" % b, align_bytes=64))

        def regroup_g(engine_copy, half):
            grouped = grp.tile([P, N_TILE, PACK], BF16, name="grouped", tag="grouped", align_bytes=64)
            engine_copy(
                out=grouped[:].rearrange("p (c i) t -> p c t i", i=4),
                in_=g_raw[:, :, half * N_TILE : (half + 1) * N_TILE].rearrange("p t (c i) -> p c t i", i=4),
            )
            return grouped

        def quantise_g(grouped, half):
            cols = slice(half * N_TILE, (half + 1) * N_TILE)
            nc.vector.quantize_mx(
                out=g_codes[:, cols].bitcast(E5M2X4),
                scales=g_scales[:, cols],
                in_=grouped[:].rearrange("p w t -> p (w t)"),
            )

        def regroup_h(b):
            grouped = grp.tile([P, ROWS, P, PACK], BF16, name="grouped", tag="grouped", align_bytes=64)
            nc.vector.tensor_copy(
                out=grouped[:].rearrange("p r i t -> p i t r"),
                in_=h_raw[b].rearrange("p t (i r) -> p i t r", r=ROWS),
            )
            return grouped

        def quantise_h(grouped, b):
            nc.vector.quantize_mx(
                out=h_codes[b][:].bitcast(E4M3X4),
                scales=h_scales[b][:],
                in_=grouped[:].rearrange("p r i t -> p (r i t)"),
            )

        g0 = regroup_g(nc.vector.tensor_copy, 0)
        g1 = regroup_g(nc.scalar.copy, 1)
        nxt = regroup_h(0)
        quantise_g(g0, 0)
        quantise_h(nxt, 0)
        quantise_g(g1, 1)

        for b in range(N_BLOCKS):
            result = stage.tile([P, ROWS, OUT_DIM], F32, name="result", tag="result")
            if b + 1 < N_BLOCKS:
                nxt = regroup_h(b + 1)
            for r in range(ROWS):
                for n in range(OUT_DIM // N_TILE):
                    acc = psum.tile([P, N_TILE], F32, name="acc", tag="acc")
                    nc.tensor.matmul_mx(
                        out=acc[:],
                        lhsT=h_codes[b][:, r * P : (r + 1) * P].bitcast(E4M3X4),
                        lhsT_scale=h_scales[b][:, r * P : (r + 1) * P],
                        rhs=g_codes[:, n * N_TILE : (n + 1) * N_TILE].bitcast(E5M2X4),
                        rhs_scale=g_scales[:, n * N_TILE : (n + 1) * N_TILE],
                        start=True,
                        stop=True,
                    )
                    dst = result[:, r, n * N_TILE : (n + 1) * N_TILE]
                    if 2 * r + n in VECTOR_BANKS:
                        nc.vector.tensor_copy(out=dst, in_=acc[:])
                    else:
                        nc.scalar.copy(out=dst, in_=acc[:])
                if r == 1 and b + 1 < N_BLOCKS:
                    quantise_h(nxt, b + 1)
                if b == 0:
                    nc.sync.dma_start(out=out_view[b][:, r, :], in_=result[:, r, :])
            if b > 0:
                nc.sync.dma_start(out=out_view[b], in_=result[:])
